import numpy as np
import ml_dtypes


def mxq(x, axis, fmt="e4m3"):
    dtype, down = {"e4m3": (ml_dtypes.float8_e4m3fn, 7), "e5m2": (ml_dtypes.float8_e5m2, 14)}[fmt]
    v = np.moveaxis(np.asarray(x, np.float32).astype(ml_dtypes.bfloat16).astype(np.float64), axis, -1)
    blocks = v.reshape(v.shape[:-1] + (-1, 32))
    amax = np.abs(blocks).max(-1, keepdims=True)
    byte = np.maximum(np.where(amax > 0, np.frexp(amax)[1] - 1 + 127, 0) - down, 1)
    scale = np.exp2(byte - 127.0)
    codes = (blocks / scale).astype(np.float32).astype(dtype).astype(np.float64)
    return np.moveaxis((codes * scale).reshape(v.shape), -1, axis)


WIDE = False


def mx_kscale(k):
    if not WIDE:
        return np.ones(k)
    levels = np.array([20, -20, 10, -10, 0])
    a = np.random.permutation(np.resize(levels, k // 512 * 4)).reshape(k // 512, 4)
    idx = np.arange(k)
    return np.exp2(a[idx // 512, idx % 128 // 32])


BF16 = ml_dtypes.bfloat16


def bf(x):
    return np.asarray(x, np.float32).astype(BF16)


def f64(x):
    return np.asarray(x).astype(np.float64)


B, N, H, T1 = 2, 3584, 512, 3072


def sigmoid(x):
    return 1.0 / (1.0 + np.exp(-x))


def setup_inputs():
    s = np.ones((B, N, 1))
    s[:, :T1] = np.asarray(mx_kscale(B * T1)).reshape(B, T1, 1)
    w = 1.0 / np.sqrt(H)
    hidden_states = bf(np.random.standard_normal((B, N, H)))
    acc0 = bf(np.random.standard_normal((B, N, H)))
    Wu_inter = bf(np.random.standard_normal((H, H)) * w)
    bu_inter = bf(np.random.standard_normal(H) * 0.3)
    Wt_inter = bf(np.random.standard_normal((H, H)) * w)
    bt_inter = bf(np.random.standard_normal(H) * 0.3)
    Wu_out = bf(np.random.standard_normal((H, H)) * w)
    bu_out = bf(np.random.standard_normal(H) * 0.3)
    Wt_out = bf(np.random.standard_normal((H, H)) * w)
    bt_out = bf(np.random.standard_normal(H) * 0.3)
    step_size = bf(0.5 + 0.5 * np.random.uniform(size=(1,)))
    g = bf(np.random.standard_normal((B, N, H)) * np.exp2(np.random.randint(-12, 1, (B, N, 1))) / s)
    zt = f64(hidden_states)[:, :T1] @ f64(Wt_inter).T + f64(bt_inter)
    return {"hidden_states": hidden_states,
            "acc": bf(f64(acc0) * s),
            "Wu_inter": Wu_inter,
            "bu_inter": bu_inter,
            "Wt_inter": Wt_inter,
            "bt_inter": bt_inter,
            "Wu_out": Wu_out,
            "bu_out": bu_out,
            "Wt_out": Wt_out,
            "bt_out": bt_out,
            "step_size": step_size,
            "zt_inter": np.asarray(zt, np.float32),
            "grad_out": g}


def reference(hidden_states, acc, Wu_inter, bu_inter, Wt_inter, bt_inter, Wu_out, bu_out, Wt_out, bt_out, step_size, zt_inter, grad_out):
    dt = 2.0 * sigmoid(f64(zt_inter)) - 1.0
    du = f64(grad_out)[:, :T1] * f64(step_size) * dt
    du = du.reshape(B * T1, H)
    a = f64(acc)[:, :T1].reshape(B * T1, H)
    return mxq(du, 0, "e5m2").T @ mxq(a, 0, "e4m3")

@@ -1,0 +1,136 @@
+from contextlib import ExitStack
+
+import concourse.mybir as mybir
+
+F32 = mybir.dt.float32
+BF16 = mybir.dt.bfloat16
+U32 = mybir.dt.uint32
+U8 = mybir.dt.uint8
+E4M3_X4 = mybir.dt.float8_e4m3fn_x4
+E5M2_X4 = mybir.dt.float8_e5m2_x4
+MULT = mybir.AluOpType.mult
+TANH = mybir.ActivationFunctionType.Tanh
+
+P = 128
+PACK = 4
+K_PASS = P * PACK
+BATCH = 2
+INTER = 3072
+H = 512
+PASSES_PER_BATCH = INTER // K_PASS
+PASSES = BATCH * PASSES_PER_BATCH
+M_TILES = H // P
+
+A_COLS_ON_VECTOR = 128
+
+FLOPS = 2 * BATCH * INTER * H * H
+BYTES = BATCH * INTER * H * (4 + 2 + 2) + H * H * 4 + 2
+
+
+def regroup(copy, grouped, raw, cols):
+    copy(
+        out=grouped[:, cols, :].rearrange("p (c i) j -> p c j i", i=4),
+        in_=raw[:, :, cols].rearrange("p j (c i) -> p c j i", i=4),
+    )
+
+
+def tile_dynamicattentionnetwork_pb_t_v_kernel(
+    tc,
+    hidden_states,
+    acc,
+    Wu_inter,
+    bu_inter,
+    Wt_inter,
+    bt_inter,
+    Wu_out,
+    bu_out,
+    Wt_out,
+    bt_out,
+    step_size,
+    zt_inter,
+    grad_out,
+    out,
+):
+    nc = tc.nc
+    with ExitStack() as ctx:
+        consts = ctx.enter_context(tc.tile_pool(name="consts", bufs=1))
+        loads = ctx.enter_context(tc.tile_pool(name="loads", bufs=6))
+        work = ctx.enter_context(tc.tile_pool(name="work", bufs=3))
+        results = ctx.enter_context(tc.tile_pool(name="results", bufs=1))
+        psum = ctx.enter_context(tc.psum_pool(name="psum", bufs=1))
+
+        step_bf16 = consts.tile([P, 1], BF16)
+        nc.scalar.dma_start(out=step_bf16[:], in_=step_size.partition_broadcast(P))
+        step = consts.tile([P, 1], F32)
+        nc.vector.tensor_copy(out=step[:], in_=step_bf16[:])
+
+        sums = [psum.tile([P, H], F32, name="sums%d" % m) for m in range(M_TILES)]
+
+        for c in range(PASSES):
+            b, r = divmod(c, PASSES_PER_BATCH)
+            tokens = slice(r * K_PASS, (r + 1) * K_PASS)
+
+            zt_raw = loads.tile([P, PACK, H], F32)
+            nc.sync.dma_start(
+                out=zt_raw[:], in_=zt_inter[b, tokens, :].rearrange("(p j) w -> p j w", j=PACK)
+            )
+            g_raw = loads.tile([P, PACK, H], BF16)
+            nc.sync.dma_start(
+                out=g_raw[:], in_=grad_out[b, tokens, :].rearrange("(p j) w -> p j w", j=PACK)
+            )
+            a_raw = loads.tile([P, PACK, H], BF16)
+            nc.sync.dma_start(
+                out=a_raw[:], in_=acc[b, tokens, :].rearrange("(p j) w -> p j w", j=PACK)
+            )
+
+            gate = work.tile([P, PACK, H], F32)
+            nc.scalar.activation(out=gate[:], in_=zt_raw[:], func=TANH, scale=0.5)
+
+            du_grouped = work.tile([P, H, PACK], BF16, align_bytes=64)
+            nc.vector.scalar_tensor_tensor(
+                out=du_grouped[:],
+                in0=gate[:].rearrange("p j w -> p w j"),
+                scalar=step[:, 0:1],
+                in1=g_raw[:].rearrange("p j w -> p w j"),
+                op0=MULT,
+                op1=MULT,
+            )
+
+            a_grouped = work.tile([P, H, PACK], BF16, align_bytes=64)
+            regroup(nc.vector.tensor_copy, a_grouped, a_raw, slice(0, A_COLS_ON_VECTOR))
+            regroup(nc.scalar.copy, a_grouped, a_raw, slice(A_COLS_ON_VECTOR, H))
+
+            du_codes = work.tile([P, H], U32, align_bytes=64)
+            du_scales = work.tile([P, H], U8, align_bytes=64)
+            nc.vector.quantize_mx(
+                out=du_codes[:].bitcast(E5M2_X4),
+                scales=du_scales[:],
+                in_=du_grouped[:].rearrange("p w j -> p (w j)"),
+            )
+            a_codes = work.tile([P, H], U32, align_bytes=64)
+            a_scales = work.tile([P, H], U8, align_bytes=64)
+            nc.vector.quantize_mx(
+                out=a_codes[:].bitcast(E4M3_X4),
+                scales=a_scales[:],
+                in_=a_grouped[:].rearrange("p w j -> p (w j)"),
+            )
+
+            for m in range(M_TILES):
+                rows = slice(m * P, (m + 1) * P)
+                nc.tensor.matmul_mx(
+                    out=sums[m][:],
+                    lhsT=du_codes[:, rows].bitcast(E5M2_X4),
+                    lhsT_scale=du_scales[:, rows],
+                    rhs=a_codes[:].bitcast(E4M3_X4),
+                    rhs_scale=a_scales[:],
+                    start=(c == 0),
+                    stop=(c == PASSES - 1),
+                )
+
+        for m in range(M_TILES):
+            result = results.tile([P, H], F32, name="result%d" % m)
+            if m % 2 == 0:
+                nc.vector.tensor_copy(out=result[:], in_=sums[m][:])
+            else:
+                nc.scalar.copy(out=result[:], in_=sums[m][:])
+            nc.sync.dma_start(out=out[m * P : (m + 1) * P, :], in_=result[:])

@@ -22,16 +22,11 @@ PASSES = BATCH * PASSES_PER_BATCH
 M_TILES = H // P
 
 A_COLS_ON_VECTOR = 128
+LOOKAHEAD = 5
+SPREAD_COLS = 32
 
 FLOPS = 2 * BATCH * INTER * H * H
 BYTES = BATCH * INTER * H * (4 + 2 + 2) + H * H * 4 + 2
-
-
-def regroup(copy, grouped, raw, cols):
-    copy(
-        out=grouped[:, cols, :].rearrange("p (c i) j -> p c j i", i=4),
-        in_=raw[:, :, cols].rearrange("p j (c i) -> p c j i", i=4),
-    )
 
 
 def tile_dynamicattentionnetwork_pb_t_v_kernel(
@@ -54,66 +49,97 @@ def tile_dynamicattentionnetwork_pb_t_v_kernel(
     nc = tc.nc
     with ExitStack() as ctx:
         consts = ctx.enter_context(tc.tile_pool(name="consts", bufs=1))
-        loads = ctx.enter_context(tc.tile_pool(name="loads", bufs=6))
+        loads = ctx.enter_context(tc.tile_pool(name="loads", bufs=LOOKAHEAD + 1))
         work = ctx.enter_context(tc.tile_pool(name="work", bufs=3))
         results = ctx.enter_context(tc.tile_pool(name="results", bufs=1))
         psum = ctx.enter_context(tc.psum_pool(name="psum", bufs=1))
+        ctx.enter_context(tc.manual_schedule())
 
-        step_bf16 = consts.tile([P, 1], BF16)
-        nc.scalar.dma_start(out=step_bf16[:], in_=step_size.partition_broadcast(P))
+        def load_pass(c):
+            b, r = divmod(c, PASSES_PER_BATCH)
+            tokens = slice(r * K_PASS, (r + 1) * K_PASS)
+            a_raw = loads.tile([P, PACK, H], BF16)
+            zt_raw = loads.tile([P, PACK, H], F32)
+            g_raw = loads.tile([P, PACK, H], BF16)
+            for raw, source in ((a_raw, acc), (zt_raw, zt_inter), (g_raw, grad_out)):
+                nc.sync.dma_start(
+                    out=raw[:], in_=source[b, tokens, :].rearrange("(p j) w -> p j w", j=PACK)
+                )
+            return a_raw, zt_raw, g_raw
+
+        loaded = [load_pass(c) for c in range(LOOKAHEAD)]
+
+        step_row = consts.tile([P, SPREAD_COLS], BF16)
+        nc.vector.memset(step_row[:], 0.0)
+        nc.scalar.dma_start(out=step_row[0:1, 0:1], in_=step_size.unsqueeze(0))
+        row0_ones = consts.tile([P, P], BF16)
+        nc.vector.memset(row0_ones[:], 0.0)
+        nc.vector.memset(row0_ones[0:1, :], 1.0)
+        step_spread = psum.tile([P, SPREAD_COLS], F32)
+        nc.tensor.matmul(out=step_spread[:], lhsT=row0_ones[:], rhs=step_row[:], start=True, stop=True)
         step = consts.tile([P, 1], F32)
-        nc.vector.tensor_copy(out=step[:], in_=step_bf16[:])
+        nc.vector.tensor_copy(out=step[:], in_=step_spread[:, 0:1])
 
         sums = [psum.tile([P, H], F32, name="sums%d" % m) for m in range(M_TILES)]
 
         for c in range(PASSES):
-            b, r = divmod(c, PASSES_PER_BATCH)
-            tokens = slice(r * K_PASS, (r + 1) * K_PASS)
-
-            zt_raw = loads.tile([P, PACK, H], F32)
-            nc.sync.dma_start(
-                out=zt_raw[:], in_=zt_inter[b, tokens, :].rearrange("(p j) w -> p j w", j=PACK)
-            )
-            g_raw = loads.tile([P, PACK, H], BF16)
-            nc.sync.dma_start(
-                out=g_raw[:], in_=grad_out[b, tokens, :].rearrange("(p j) w -> p j w", j=PACK)
-            )
-            a_raw = loads.tile([P, PACK, H], BF16)
-            nc.sync.dma_start(
-                out=a_raw[:], in_=acc[b, tokens, :].rearrange("(p j) w -> p j w", j=PACK)
-            )
-
-            gate = work.tile([P, PACK, H], F32)
-            nc.scalar.activation(out=gate[:], in_=zt_raw[:], func=TANH, scale=0.5)
-
-            du_grouped = work.tile([P, H, PACK], BF16, align_bytes=64)
-            nc.vector.scalar_tensor_tensor(
-                out=du_grouped[:],
-                in0=gate[:].rearrange("p j w -> p w j"),
-                scalar=step[:, 0:1],
-                in1=g_raw[:].rearrange("p j w -> p w j"),
-                op0=MULT,
-                op1=MULT,
-            )
+            if c + LOOKAHEAD < PASSES:
+                loaded.append(load_pass(c + LOOKAHEAD))
+            a_raw, zt_raw, g_raw = loaded[c]
+            last = c == PASSES - 1
 
             a_grouped = work.tile([P, H, PACK], BF16, align_bytes=64)
-            regroup(nc.vector.tensor_copy, a_grouped, a_raw, slice(0, A_COLS_ON_VECTOR))
-            regroup(nc.scalar.copy, a_grouped, a_raw, slice(A_COLS_ON_VECTOR, H))
-
-            du_codes = work.tile([P, H], U32, align_bytes=64)
-            du_scales = work.tile([P, H], U8, align_bytes=64)
-            nc.vector.quantize_mx(
-                out=du_codes[:].bitcast(E5M2_X4),
-                scales=du_scales[:],
-                in_=du_grouped[:].rearrange("p w j -> p (w j)"),
-            )
+            for copy, cols in (
+                (nc.vector.tensor_copy, slice(0, A_COLS_ON_VECTOR)),
+                (nc.scalar.copy, slice(A_COLS_ON_VECTOR, H)),
+            ):
+                copy(
+                    out=a_grouped[:, cols, :].rearrange("p (c i) j -> p c j i", i=4),
+                    in_=a_raw[:, :, cols].rearrange("p j (c i) -> p c j i", i=4),
+                )
             a_codes = work.tile([P, H], U32, align_bytes=64)
             a_scales = work.tile([P, H], U8, align_bytes=64)
+
+            pieces = M_TILES if last else 1
+            width = H // pieces
+            piece_cols = [slice(i * width, (i + 1) * width) for i in range(pieces)]
+            gate = work.tile([P, PACK, H], F32)
+            du_grouped = work.tile([P, H, PACK], BF16, align_bytes=64)
+            du_codes = work.tile([P, H], U32, align_bytes=64)
+            du_scales = work.tile([P, H], U8, align_bytes=64)
+
+            def multiply(cols):
+                nc.vector.scalar_tensor_tensor(
+                    out=du_grouped[:, cols, :],
+                    in0=gate[:, :, cols].rearrange("p j w -> p w j"),
+                    scalar=step[:, 0:1],
+                    in1=g_raw[:, :, cols].rearrange("p j w -> p w j"),
+                    op0=MULT,
+                    op1=MULT,
+                )
+
+            def quantise_du(cols):
+                nc.vector.quantize_mx(
+                    out=du_codes[:, cols].bitcast(E5M2_X4),
+                    scales=du_scales[:, cols],
+                    in_=du_grouped[:, cols, :].rearrange("p w j -> p (w j)"),
+                )
+
+            for cols in piece_cols:
+                nc.scalar.activation(
+                    out=gate[:, :, cols], in_=zt_raw[:, :, cols], func=TANH, scale=0.5
+                )
+
+            multiply(piece_cols[0])
             nc.vector.quantize_mx(
                 out=a_codes[:].bitcast(E4M3_X4),
                 scales=a_scales[:],
                 in_=a_grouped[:].rearrange("p w j -> p (w j)"),
             )
+            for i in range(1, pieces):
+                multiply(piece_cols[i])
+                quantise_du(piece_cols[i - 1])
+            quantise_du(piece_cols[pieces - 1])
 
             for m in range(M_TILES):
                 rows = slice(m * P, (m + 1) * P)
@@ -124,13 +150,13 @@ def tile_dynamicattentionnetwork_pb_t_v_kernel(
                     rhs=a_codes[:].bitcast(E4M3_X4),
                     rhs_scale=a_scales[:],
                     start=(c == 0),
-                    stop=(c == PASSES - 1),
+                    stop=last,
                 )
 
         for m in range(M_TILES):
             result = results.tile([P, H], F32, name="result%d" % m)
-            if m % 2 == 0:
-                nc.vector.tensor_copy(out=result[:], in_=sums[m][:])
-            else:
+            if m < M_TILES - 1:
                 nc.scalar.copy(out=result[:], in_=sums[m][:])
+            else:
+                nc.vector.tensor_copy(out=result[:], in_=sums[m][:])
             nc.sync.dma_start(out=out[m * P : (m + 1) * P, :], in_=result[:])

@@ -89,10 +89,10 @@ def tile_dynamicattentionnetwork_pb_t_v_kernel(
             last = c == PASSES - 1
 
             a_grouped = work.tile([P, H, PACK], BF16, align_bytes=64)
-            for copy, cols in (
-                (nc.vector.tensor_copy, slice(0, A_COLS_ON_VECTOR)),
-                (nc.scalar.copy, slice(A_COLS_ON_VECTOR, H)),
-            ):
+            shares = [(nc.scalar.copy, slice(0 if last else A_COLS_ON_VECTOR, H))]
+            if not last:
+                shares.append((nc.vector.tensor_copy, slice(0, A_COLS_ON_VECTOR)))
+            for copy, cols in shares:
                 copy(
                     out=a_grouped[:, cols, :].rearrange("p (c i) j -> p c j i", i=4),
                     in_=a_raw[:, :, cols].rearrange("p j (c i) -> p c j i", i=4),
@@ -130,12 +130,18 @@ def tile_dynamicattentionnetwork_pb_t_v_kernel(
                     out=gate[:, :, cols], in_=zt_raw[:, :, cols], func=TANH, scale=0.5
                 )
 
+            def quantise_a():
+                nc.vector.quantize_mx(
+                    out=a_codes[:].bitcast(E4M3_X4),
+                    scales=a_scales[:],
+                    in_=a_grouped[:].rearrange("p w j -> p (w j)"),
+                )
+
+            if last:
+                quantise_a()
             multiply(piece_cols[0])
-            nc.vector.quantize_mx(
-                out=a_codes[:].bitcast(E4M3_X4),
-                scales=a_scales[:],
-                in_=a_grouped[:].rearrange("p w j -> p (w j)"),
-            )
+            if not last:
+                quantise_a()
             for i in range(1, pieces):
                 multiply(piece_cols[i])
                 quantise_du(piece_cols[i - 1])

@@ -21,7 +21,7 @@ PASSES_PER_BATCH = INTER // K_PASS
 PASSES = BATCH * PASSES_PER_BATCH
 M_TILES = H // P
 
-A_COLS_ON_VECTOR = 128
+A_COLS_ON_VECTOR = 0
 LOOKAHEAD = 5
 SPREAD_COLS = 32
 
@@ -90,7 +90,7 @@ def tile_dynamicattentionnetwork_pb_t_v_kernel(
 
             a_grouped = work.tile([P, H, PACK], BF16, align_bytes=64)
             shares = [(nc.scalar.copy, slice(0 if last else A_COLS_ON_VECTOR, H))]
-            if not last:
+            if not last and A_COLS_ON_VECTOR > 0:
                 shares.append((nc.vector.tensor_copy, slice(0, A_COLS_ON_VECTOR)))
             for copy, cols in shares:
                 copy(

@@ -61,7 +61,10 @@ def tile_dynamicattentionnetwork_pb_t_v_kernel(
             a_raw = loads.tile([P, PACK, H], BF16)
             zt_raw = loads.tile([P, PACK, H], F32)
             g_raw = loads.tile([P, PACK, H], BF16)
-            for raw, source in ((a_raw, acc), (zt_raw, zt_inter), (g_raw, grad_out)):
+            order = [(zt_raw, zt_inter), (a_raw, acc), (g_raw, grad_out)]
+            if c == PASSES - 1:
+                order = [(a_raw, acc), (zt_raw, zt_inter), (g_raw, grad_out)]
+            for raw, source in order:
                 nc.sync.dma_start(
                     out=raw[:], in_=source[b, tokens, :].rearrange("(p j) w -> p j w", j=PACK)
                 )
@@ -89,14 +92,13 @@ def tile_dynamicattentionnetwork_pb_t_v_kernel(
             last = c == PASSES - 1
 
             a_grouped = work.tile([P, H, PACK], BF16, align_bytes=64)
-            shares = [(nc.scalar.copy, slice(0 if last else A_COLS_ON_VECTOR, H))]
-            if not last and A_COLS_ON_VECTOR > 0:
-                shares.append((nc.vector.tensor_copy, slice(0, A_COLS_ON_VECTOR)))
-            for copy, cols in shares:
-                copy(
-                    out=a_grouped[:, cols, :].rearrange("p (c i) j -> p c j i", i=4),
-                    in_=a_raw[:, :, cols].rearrange("p j (c i) -> p c j i", i=4),
+
+            def regroup_a():
+                nc.scalar.copy(
+                    out=a_grouped[:].rearrange("p (c i) j -> p c j i", i=4),
+                    in_=a_raw[:].rearrange("p j (c i) -> p c j i", i=4),
                 )
+
             a_codes = work.tile([P, H], U32, align_bytes=64)
             a_scales = work.tile([P, H], U8, align_bytes=64)
 
@@ -125,10 +127,14 @@ def tile_dynamicattentionnetwork_pb_t_v_kernel(
                     in_=du_grouped[:, cols, :].rearrange("p w j -> p (w j)"),
                 )
 
+            if last:
+                regroup_a()
             for cols in piece_cols:
                 nc.scalar.activation(
                     out=gate[:, :, cols], in_=zt_raw[:, :, cols], func=TANH, scale=0.5
                 )
+            if not last:
+                regroup_a()
 
             def quantise_a():
                 nc.vector.quantize_mx(

@@ -106,6 +106,7 @@ def tile_dynamicattentionnetwork_pb_t_v_kernel(
             width = H // pieces
             piece_cols = [slice(i * width, (i + 1) * width) for i in range(pieces)]
             gate = work.tile([P, PACK, H], F32)
+            gate_grouped = gate[:].rearrange("p j w -> p (j w)").rearrange("p (w j) -> p w j", j=PACK)
             du_grouped = work.tile([P, H, PACK], BF16, align_bytes=64)
             du_codes = work.tile([P, H], U32, align_bytes=64)
             du_scales = work.tile([P, H], U8, align_bytes=64)
@@ -113,7 +114,7 @@ def tile_dynamicattentionnetwork_pb_t_v_kernel(
             def multiply(cols):
                 nc.vector.scalar_tensor_tensor(
                     out=du_grouped[:, cols, :],
-                    in0=gate[:, :, cols].rearrange("p j w -> p w j"),
+                    in0=gate_grouped[:, cols, :] if last else gate[:, :, cols].rearrange("p j w -> p w j"),
                     scalar=step[:, 0:1],
                     in1=g_raw[:, :, cols].rearrange("p j w -> p w j"),
                     op0=MULT,
@@ -130,9 +131,17 @@ def tile_dynamicattentionnetwork_pb_t_v_kernel(
             if last:
                 regroup_a()
             for cols in piece_cols:
-                nc.scalar.activation(
-                    out=gate[:, :, cols], in_=zt_raw[:, :, cols], func=TANH, scale=0.5
-                )
+                if last:
+                    nc.scalar.activation(
+                        out=gate_grouped[:, cols, :].rearrange("p (c i) j -> p c j i", i=4),
+                        in_=zt_raw[:, :, cols].rearrange("p j (c i) -> p c j i", i=4),
+                        func=TANH,
+                        scale=0.5,
+                    )
+                else:
+                    nc.scalar.activation(
+                        out=gate[:, :, cols], in_=zt_raw[:, :, cols], func=TANH, scale=0.5
+                    )
             if not last:
                 regroup_a()
 

@@ -95,8 +95,8 @@ def tile_dynamicattentionnetwork_pb_t_v_kernel(
 
             def regroup_a():
                 nc.scalar.copy(
-                    out=a_grouped[:].rearrange("p (c i) j -> p c j i", i=4),
-                    in_=a_raw[:].rearrange("p j (c i) -> p c j i", i=4),
+                    out=a_grouped[:].rearrange("p (c i) j -> p c j i", i=8),
+                    in_=a_raw[:].rearrange("p j (c i) -> p c j i", i=8),
                 )
 
             a_codes = work.tile([P, H], U32, align_bytes=64)

from contextlib import ExitStack

import concourse.mybir as mybir

F32 = mybir.dt.float32
BF16 = mybir.dt.bfloat16
U32 = mybir.dt.uint32
U8 = mybir.dt.uint8
E4M3_X4 = mybir.dt.float8_e4m3fn_x4
E5M2_X4 = mybir.dt.float8_e5m2_x4
MULT = mybir.AluOpType.mult
TANH = mybir.ActivationFunctionType.Tanh

P = 128
PACK = 4
K_PASS = P * PACK
BATCH = 2
INTER = 3072
H = 512
PASSES_PER_BATCH = INTER // K_PASS
PASSES = BATCH * PASSES_PER_BATCH
M_TILES = H // P

A_COLS_ON_VECTOR = 0
LOOKAHEAD = 5
SPREAD_COLS = 32

FLOPS = 2 * BATCH * INTER * H * H
BYTES = BATCH * INTER * H * (4 + 2 + 2) + H * H * 4 + 2


def tile_dynamicattentionnetwork_pb_t_v_kernel(
    tc,
    hidden_states,
    acc,
    Wu_inter,
    bu_inter,
    Wt_inter,
    bt_inter,
    Wu_out,
    bu_out,
    Wt_out,
    bt_out,
    step_size,
    zt_inter,
    grad_out,
    out,
):
    nc = tc.nc
    with ExitStack() as ctx:
        consts = ctx.enter_context(tc.tile_pool(name="consts", bufs=1))
        loads = ctx.enter_context(tc.tile_pool(name="loads", bufs=LOOKAHEAD + 1))
        work = ctx.enter_context(tc.tile_pool(name="work", bufs=3))
        results = ctx.enter_context(tc.tile_pool(name="results", bufs=1))
        psum = ctx.enter_context(tc.psum_pool(name="psum", bufs=1))
        ctx.enter_context(tc.manual_schedule())

        def load_pass(c):
            b, r = divmod(c, PASSES_PER_BATCH)
            tokens = slice(r * K_PASS, (r + 1) * K_PASS)
            a_raw = loads.tile([P, PACK, H], BF16)
            zt_raw = loads.tile([P, PACK, H], F32)
            g_raw = loads.tile([P, PACK, H], BF16)
            order = [(zt_raw, zt_inter), (a_raw, acc), (g_raw, grad_out)]
            if c == PASSES - 1:
                order = [(a_raw, acc), (zt_raw, zt_inter), (g_raw, grad_out)]
            for raw, source in order:
                nc.sync.dma_start(
                    out=raw[:], in_=source[b, tokens, :].rearrange("(p j) w -> p j w", j=PACK)
                )
            return a_raw, zt_raw, g_raw

        loaded = [load_pass(c) for c in range(LOOKAHEAD)]

        step_row = consts.tile([P, SPREAD_COLS], BF16)
        nc.vector.memset(step_row[:], 0.0)
        nc.scalar.dma_start(out=step_row[0:1, 0:1], in_=step_size.unsqueeze(0))
        row0_ones = consts.tile([P, P], BF16)
        nc.vector.memset(row0_ones[:], 0.0)
        nc.vector.memset(row0_ones[0:1, :], 1.0)
        step_spread = psum.tile([P, SPREAD_COLS], F32)
        nc.tensor.matmul(out=step_spread[:], lhsT=row0_ones[:], rhs=step_row[:], start=True, stop=True)
        step = consts.tile([P, 1], F32)
        nc.vector.tensor_copy(out=step[:], in_=step_spread[:, 0:1])

        sums = [psum.tile([P, H], F32, name="sums%d" % m) for m in range(M_TILES)]

        for c in range(PASSES):
            if c + LOOKAHEAD < PASSES:
                loaded.append(load_pass(c + LOOKAHEAD))
            a_raw, zt_raw, g_raw = loaded[c]
            last = c == PASSES - 1

            a_grouped = work.tile([P, H, PACK], BF16, align_bytes=64)

            def regroup_a():
                nc.scalar.copy(
                    out=a_grouped[:].rearrange("p (c i) j -> p c j i", i=8),
                    in_=a_raw[:].rearrange("p j (c i) -> p c j i", i=8),
                )

            a_codes = work.tile([P, H], U32, align_bytes=64)
            a_scales = work.tile([P, H], U8, align_bytes=64)

            pieces = M_TILES if last else 1
            width = H // pieces
            piece_cols = [slice(i * width, (i + 1) * width) for i in range(pieces)]
            gate = work.tile([P, PACK, H], F32)
            gate_grouped = gate[:].rearrange("p j w -> p (j w)").rearrange("p (w j) -> p w j", j=PACK)
            du_grouped = work.tile([P, H, PACK], BF16, align_bytes=64)
            du_codes = work.tile([P, H], U32, align_bytes=64)
            du_scales = work.tile([P, H], U8, align_bytes=64)

            def multiply(cols):
                nc.vector.scalar_tensor_tensor(
                    out=du_grouped[:, cols, :],
                    in0=gate_grouped[:, cols, :] if last else gate[:, :, cols].rearrange("p j w -> p w j"),
                    scalar=step[:, 0:1],
                    in1=g_raw[:, :, cols].rearrange("p j w -> p w j"),
                    op0=MULT,
                    op1=MULT,
                )

            def quantise_du(cols):
                nc.vector.quantize_mx(
                    out=du_codes[:, cols].bitcast(E5M2_X4),
                    scales=du_scales[:, cols],
                    in_=du_grouped[:, cols, :].rearrange("p w j -> p (w j)"),
                )

            if last:
                regroup_a()
            for cols in piece_cols:
                if last:
                    nc.scalar.activation(
                        out=gate_grouped[:, cols, :].rearrange("p (c i) j -> p c j i", i=4),
                        in_=zt_raw[:, :, cols].rearrange("p j (c i) -> p c j i", i=4),
                        func=TANH,
                        scale=0.5,
                    )
                else:
                    nc.scalar.activation(
                        out=gate[:, :, cols], in_=zt_raw[:, :, cols], func=TANH, scale=0.5
                    )
            if not last:
                regroup_a()

            def quantise_a():
                nc.vector.quantize_mx(
                    out=a_codes[:].bitcast(E4M3_X4),
                    scales=a_scales[:],
                    in_=a_grouped[:].rearrange("p w j -> p (w j)"),
                )

            if last:
                quantise_a()
            multiply(piece_cols[0])
            if not last:
                quantise_a()
            for i in range(1, pieces):
                multiply(piece_cols[i])
                quantise_du(piece_cols[i - 1])
            quantise_du(piece_cols[pieces - 1])

            for m in range(M_TILES):
                rows = slice(m * P, (m + 1) * P)
                nc.tensor.matmul_mx(
                    out=sums[m][:],
                    lhsT=du_codes[:, rows].bitcast(E5M2_X4),
                    lhsT_scale=du_scales[:, rows],
                    rhs=a_codes[:].bitcast(E4M3_X4),
                    rhs_scale=a_scales[:],
                    start=(c == 0),
                    stop=last,
                )

        for m in range(M_TILES):
            result = results.tile([P, H], F32, name="result%d" % m)
            if m < M_TILES - 1:
                nc.scalar.copy(out=result[:], in_=sums[m][:])
            else:
                nc.vector.tensor_copy(out=result[:], in_=sums[m][:])
            nc.sync.dma_start(out=out[m * P : (m + 1) * P, :], in_=result[:])
